import numpy as np
import ml_dtypes


BF16 = ml_dtypes.bfloat16


def bf(x):
    return np.asarray(x, np.float32).astype(BF16)


def f64(x):
    return np.asarray(x).astype(np.float64)


E2M1 = np.array([0.0, 0.5, 1.0, 1.5, 2.0, 3.0, 4.0, 6.0, -0.0, -0.5, -1.0, -1.5, -2.0, -3.0, -4.0, -6.0])


def pack_weight(w, fmt):
    k, n = w.shape
    w = f64(bf(w)).reshape(k // 32, 32, n)
    amax = np.abs(w).max(1)
    if fmt == "e4m3":
        byte = np.frexp(amax)[1] - 1 + 127 - 7
    else:
        mant, ex = np.frexp(amax / 6.0)
        byte = np.where(mant > 0.5, ex, ex - 1) + 127
    byte = np.clip(np.where(amax > 0, byte, 1), 1, 254)
    scaled = (w * np.exp2(127.0 - byte)[:, None, :]).reshape(k, n).astype(np.float32)
    by_word = np.ascontiguousarray(scaled.reshape(k // 512, 128, 4, n).transpose(0, 1, 3, 2))
    if fmt == "e4m3":
        words = by_word.astype(ml_dtypes.float8_e4m3fn).view(np.uint8)
    else:
        c = by_word.astype(ml_dtypes.float4_e2m1fn).view(np.uint8) & 0xF
        words = c[..., 0::2] | (c[..., 1::2] << 4)
    return np.ascontiguousarray(words), np.ascontiguousarray(byte.astype(np.uint8).reshape(k // 512, 16, n))


def unpack_weight(words, scales, fmt):
    g, p, n, _ = words.shape
    if fmt == "e4m3":
        vals = np.ascontiguousarray(words).view(ml_dtypes.float8_e4m3fn).astype(np.float64)
    else:
        nib = np.empty((g, p, n, 4), np.uint8)
        nib[..., 0::2] = words & 0xF
        nib[..., 1::2] = words >> 4
        vals = E2M1[nib]
    vals = vals * np.repeat(np.exp2(scales.astype(np.float64) - 127.0), 8, axis=1)[..., None]
    return vals.transpose(0, 1, 3, 2).reshape(g * 512, n)

def pack4(w):
    words, scales = pack_weight(w, "e2m1")
    return words.reshape(words.shape[0], 128, -1), scales


def unpack4(words, scales):
    return unpack_weight(words.reshape(words.shape[0], 128, -1, 2), scales, "e2m1")


def kspread(k):
    return np.exp2(np.repeat(np.random.randint(-6, 7, k // 32), 32).astype(np.float64))


B, T, C, NH, G, HS, K, WIN = 1, 2048, 4096, 16, 4, 128, 4, 512
QPK = NH // G


def silu(v):
    return v / (1.0 + np.exp(-v))


def causal_conv1d_silu(u, w):
    up = np.pad(u, ((0, 0), (K - 1, 0), (0, 0)))
    out = sum(w[None, None, :, j] * up[:, j:j + T, :] for j in range(K))
    return silu(out)


def apply_rope(u, cos, sin):
    d = cos.shape[-1]
    u1, u2 = u[..., :d], u[..., d:]
    c = cos[None, :, None, :]
    s = sin[None, :, None, :]
    return np.concatenate([u1 * c - u2 * s, u1 * s + u2 * c], axis=-1)


def setup_inputs():
    s = kspread(C)
    theta = 1.0 / (10000.0 ** (np.arange(0, HS, 2) / HS))
    idx = np.outer(np.arange(T), theta)
    x = np.random.standard_normal((B, T, C)) * s
    x_words, x_scales = pack4(x.reshape(B * T, C).T)
    words, scales = pack4(np.random.standard_normal((C, (NH + 2 * G) * HS)) * 2.0 / np.sqrt(C) / s[:, None])
    return {"x_words": x_words, "x_scales": x_scales,
            "Wqkv_words": words, "Wqkv_scales": scales,
            "q_conv_w": bf(np.random.standard_normal((NH * HS, K)) * 0.5),
            "k_conv_w": bf(np.random.standard_normal((G * HS, K)) * 0.5),
            "v_conv_w": bf(np.random.standard_normal((G * HS, K)) * 0.5),
            "cos": bf(np.cos(idx)), "sin": bf(np.sin(idx))}


def reference(x_words, x_scales, Wqkv_words, Wqkv_scales, q_conv_w, k_conv_w, v_conv_w, cos, sin):
    qkv = (unpack4(x_words, x_scales).T @ unpack4(Wqkv_words, Wqkv_scales)).reshape(B, T, G, QPK + 2, HS)
    q = qkv[..., :QPK, :].reshape(B, T, NH * HS)
    k = qkv[..., QPK:QPK + 1, :].reshape(B, T, G * HS)
    v = qkv[..., QPK + 1:, :].reshape(B, T, G * HS)
    q = causal_conv1d_silu(q, f64(q_conv_w)).reshape(B, T, NH, HS)
    k = causal_conv1d_silu(k, f64(k_conv_w)).reshape(B, T, G, HS)
    v = causal_conv1d_silu(v, f64(v_conv_w)).reshape(B, T, G, HS)
    q = apply_rope(q, f64(cos), f64(sin))
    k = apply_rope(k, f64(cos), f64(sin))
    return q, k, v

@@ -1,0 +1,309 @@
+from contextlib import ExitStack
+
+import concourse.mybir as mybir
+from concourse.masks import make_identity
+
+F32 = mybir.dt.float32
+BF16 = mybir.dt.bfloat16
+U8 = mybir.dt.uint8
+I32 = mybir.dt.int32
+FP4X4 = mybir.dt.float4_e2m1fn_x4
+AF = mybir.ActivationFunctionType
+ALU = mybir.AluOpType
+
+FLOPS = 2 * 2048 * 4096 * 3072
+
+P = 128
+PASSES = 8
+NTOK = 512
+NG = 96
+ACCW = 520
+DIRECT0 = 88
+LASTU = 23
+
+SLAG = 6
+TLAG = 9
+RLAG = 10
+PLAG = 3
+ALAG = 12
+VEC, ACT = 0, 1
+
+
+def tile_gpt_pa_kernel(
+    tc, x_words, x_scales, Wqkv_words, Wqkv_scales, q_conv_w, k_conv_w, v_conv_w, cos, sin, out_0, out_1, out_2
+):
+    nc = tc.nc
+    with ExitStack() as ctx:
+        keep = ctx.enter_context(tc.tile_pool(name="keep", bufs=1))
+        work = ctx.enter_context(tc.tile_pool(name="work", bufs=2))
+        psum = ctx.enter_context(tc.psum_pool(name="psum", bufs=4))
+        ctx.enter_context(tc.manual_schedule())
+
+        xc, xp, wcq, wpq, wck, wpk = [], [], [], [], [], []
+        for b in range(4):
+            t_xc = keep.tile([P, PASSES, 1024], U8, name="xc%d" % b, align_bytes=64)
+            t_xp = keep.tile([P, PASSES, 512], U8, name="xp%d" % b, align_bytes=64)
+            t_wcq = keep.tile([P, PASSES, 1024], U8, name="wcq%d" % b, align_bytes=64)
+            t_wpq = keep.tile([P, PASSES, 512], U8, name="wpq%d" % b, align_bytes=64)
+            t_wck = keep.tile([P, PASSES, 512], U8, name="wck%d" % b, align_bytes=64)
+            t_wpk = keep.tile([P, PASSES, 256], U8, name="wpk%d" % b, align_bytes=64)
+            xc.append(t_xc)
+            xp.append(t_xp)
+            wcq.append(t_wcq)
+            wpq.append(t_wpq)
+            wck.append(t_wck)
+            wpk.append(t_wpk)
+        wl = keep.tile([P, 512], BF16, name="wl")
+        wd = keep.tile([P, 4, P], F32, name="wd")
+        wf = keep.tile([P, 4, 24], F32, name="wf")
+        craw = keep.tile([P, 16, 64], BF16, name="craw")
+        sraw = keep.tile([P, 16, 64], BF16, name="sraw")
+        cos2 = keep.tile([P, 16, 128], F32, name="cos2")
+        sinpm = keep.tile([P, 16, 128], F32, name="sinpm")
+        ident = keep.tile([P, P], F32, name="ident")
+        zeros = keep.tile([P, 8], F32, name="zeros")
+        scr = keep.tile([P, 8], F32, name="scr")
+
+        def load_codes(dst, src, g0, g1, n0, n1):
+            nc.sync.dma_start(
+                out=dst[:, g0:g1, :].bitcast(I32),
+                in_=src[g0:g1, :, 2 * n0 : 2 * n1].rearrange("g p n -> p g n").bitcast(I32),
+            )
+
+        def load_scales(dst, src, n0, n1):
+            for q in range(4):
+                nc.sync.dma_start(
+                    out=dst[32 * q : 32 * q + 4, :, :].bitcast(I32),
+                    in_=src[:, 4 * q : 4 * q + 4, n0:n1].rearrange("g r n -> r g n").bitcast(I32),
+                )
+
+        nc.vector.memset(xp[0][:].bitcast(I32), 0)
+        nc.gpsimd.memset(wpq[0][:].bitcast(F32), 0.0)
+        nc.vector.memset(wl[:], 0.0)
+        nc.gpsimd.memset(zeros[:], 0.0)
+        nc.gpsimd.dma_start(out=wl[0:16, :], in_=q_conv_w.rearrange("(h p) j -> h (p j)", p=P))
+        nc.gpsimd.dma_start(out=wl[16:20, :], in_=k_conv_w.rearrange("(h p) j -> h (p j)", p=P))
+        nc.gpsimd.dma_start(out=wl[20:24, :], in_=v_conv_w.rearrange("(h p) j -> h (p j)", p=P))
+        make_identity(nc, ident[:])
+        nc.scalar.activation(out=scr[:, 0:1], in_=zeros[:, 0:1], func=AF.Silu)
+
+        load_codes(xc[0], x_words, 0, 4, 0, 512)
+        load_codes(wcq[0], Wqkv_words, 0, 4, 0, 512)
+        load_scales(xp[0], x_scales, 0, 512)
+        load_scales(wpq[0], Wqkv_scales, 0, 512)
+        load_codes(xc[0], x_words, 4, 8, 0, 512)
+        load_codes(wcq[0], Wqkv_words, 4, 8, 0, 512)
+
+        for b in range(1, 4):
+            nc.vector.memset(xp[b][:].bitcast(I32), 0)
+            nc.gpsimd.memset(wpq[b][:].bitcast(F32), 0.0)
+        for c in range(4):
+            nc.gpsimd.memset(wpk[c][:].bitcast(F32), 0.0)
+        for b in range(1, 4):
+            load_scales(xp[b], x_scales, 512 * b, 512 * (b + 1))
+        load_codes(xc[1], x_words, 0, 8, 512, 1024)
+        nc.sync.dma_start(out=craw[:], in_=cos.rearrange("(t p) i -> p t i", p=P))
+        nc.sync.dma_start(out=sraw[:], in_=sin.rearrange("(t p) i -> p t i", p=P))
+        load_codes(xc[2], x_words, 0, 8, 1024, 1536)
+        load_codes(xc[3], x_words, 0, 8, 1536, 2048)
+        for c in range(1, 4):
+            load_scales(wpq[c], Wqkv_scales, 768 * c, 768 * c + 512)
+        for c in range(4):
+            load_scales(wpk[c], Wqkv_scales, 768 * c + 512, 768 * c + 768)
+        for c in range(1, 4):
+            load_codes(wcq[c], Wqkv_words, 0, 8, 768 * c, 768 * c + 512)
+        for c in range(4):
+            load_codes(wck[c], Wqkv_words, 0, 8, 768 * c + 512, 768 * c + 768)
+
+        nc.vector.tensor_copy(out=wd[:], in_=wl[:].rearrange("h (p j) -> h j p", j=4))
+
+        def conv_weights():
+            wt = psum.tile([P, 4, P], F32, name="tb", tag="tb", bufs=4)
+            for j in range(4):
+                nc.tensor.transpose(out=wt[:, j, :], in_=wd[:, j, :], identity=ident[:])
+            nc.vector.tensor_copy(out=wf[:], in_=wt[:, :, 0:24])
+
+        def rope_tables():
+            nc.scalar.copy(out=cos2[:, :, 0:64], in_=craw[:])
+            nc.scalar.copy(out=cos2[:, :, 64:128], in_=craw[:])
+            nc.vector.tensor_scalar_mul(out=sinpm[:, :, 0:64], in0=sraw[:], scalar1=-1.0)
+            nc.vector.tensor_copy(out=sinpm[:, :, 64:128], in_=sraw[:])
+
+        ubank, acc, tmp, tbank, stage, bst = {}, {}, {}, {}, {}, {}
+
+        def info(i):
+            st, r = divmod(i, 16)
+            b, hh = divmod(r, 4)
+            if st < 4:
+                return b, wcq[st], wpq[st], 128 * hh, 4 * st + hh
+            return b, wck[hh], wpk[hh], 128 * (st - 4), 16 + 4 * (st - 4) + hh
+
+        def pool_tap(i):
+            return i < DIRECT0
+
+        def project(i):
+            b, codes, planes, col, widx = info(i)
+            u = psum.tile([P, NTOK], F32, name="u", tag="u", bufs=4)
+            ubank[i] = u
+            for g in range(PASSES):
+                nc.tensor.matmul_mx(
+                    out=u[:],
+                    lhsT=codes[:, g, 2 * col : 2 * col + 256].bitcast(FP4X4),
+                    lhsT_scale=planes[:, g, col : col + 128],
+                    rhs=xc[b][:, g, :].bitcast(FP4X4),
+                    rhs_scale=xp[b][:, g, :],
+                    start=(g == 0),
+                    stop=(g == PASSES - 1),
+                )
+
+        def taps(i):
+            b, codes, planes, col, widx = info(i)
+            pr, e = divmod(i, 2)
+            if e == 0:
+                a_new = work.tile([P, 2, ACCW], F32, name="acc", tag="acc", bufs=6)
+                acc[pr] = a_new
+                if pool_tap(i):
+                    t_new = work.tile([P, 2, NTOK], F32, name="tmp", tag="tmp", bufs=3)
+                    tmp[pr] = t_new
+            a = acc[pr]
+            u = ubank[i]
+            if b == 0:
+                nc.scalar.copy(out=a[:, e, 0:3], in_=zeros[:, 0:3])
+            else:
+                nc.scalar.copy(out=a[:, e, 0:3], in_=acc[pr - 2][:, e, NTOK : NTOK + 3])
+            nc.scalar.activation(out=a[:, e, 3 : NTOK + 3], in_=u[:], func=AF.Copy, scale=wf[:, 0, widx : widx + 1])
+            if pool_tap(i):
+                nc.scalar.activation(out=tmp[pr][:, e, :], in_=u[:], func=AF.Copy, scale=wf[:, 3, widx : widx + 1])
+
+        def conv(i):
+            b, codes, planes, col, widx = info(i)
+            pr, e = divmod(i, 2)
+            a = acc[pr]
+            u = ubank[i]
+            for j in (1, 2) if pool_tap(i) else (1, 2, 3):
+                sh = 3 - j
+                nc.vector.scalar_tensor_tensor(
+                    out=a[:, e, sh : sh + NTOK],
+                    in0=u[:],
+                    scalar=wf[:, j, widx : widx + 1],
+                    in1=a[:, e, sh : sh + NTOK],
+                    op0=ALU.mult,
+                    op1=ALU.add,
+                )
+
+        def pool_add(pr):
+            nc.gpsimd.tensor_tensor(out=acc[pr][:, :, 0:NTOK], in0=acc[pr][:, :, 0:NTOK], in1=tmp[pr][:], op=ALU.add)
+
+        def silu_pair(pr):
+            nc.scalar.activation(out=acc[pr][:, :, 0:NTOK], in_=acc[pr][:, :, 0:NTOK], func=AF.Silu)
+
+        def silu_one(i):
+            pr, e = divmod(i, 2)
+            nc.scalar.activation(out=acc[pr][:, e, 0:NTOK], in_=acc[pr][:, e, 0:NTOK], func=AF.Silu)
+
+        def transposes(un, hh, tag):
+            tb = psum.tile([P, 4, P], F32, name=tag, tag=tag, bufs=4)
+            tbank[(un, hh)] = tb
+            a = acc[2 * un + hh // 2]
+            for tt in range(4):
+                nc.tensor.transpose(out=tb[:, tt, :], in_=a[:, hh % 2, P * tt : P * (tt + 1)], identity=ident[:])
+
+        def rotate(un, hh, copy_engine):
+            b = un % 4
+            width = 1 if un == LASTU else 2
+            key, e = (un, hh // width), hh % width
+            if key not in stage:
+                s_new = work.tile([P, 4, width, P], F32, name="stage", tag="stage", bufs=6)
+                stage[key] = s_new
+                if un < 20:
+                    b_new = work.tile([P, 4, width, P], F32, name="bst", tag="bst", bufs=4)
+                    bst[key] = b_new
+            tb = tbank[(un, hh)]
+            if un >= 20:
+                if copy_engine == VEC:
+                    nc.vector.tensor_copy(out=stage[key][:, :, e, :], in_=tb[:])
+                else:
+                    nc.scalar.copy(out=stage[key][:, :, e, :], in_=tb[:])
+                return
+            tts = slice(4 * b, 4 * b + 4)
+            nc.vector.tensor_tensor(out=stage[key][:, :, e, :], in0=tb[:], in1=cos2[:, tts, :], op=ALU.mult)
+            nc.vector.tensor_tensor(
+                out=bst[key][:, :, e, 0:64], in0=tb[:, :, 64:128], in1=sinpm[:, tts, 0:64], op=ALU.mult
+            )
+            nc.vector.tensor_tensor(
+                out=bst[key][:, :, e, 64:128], in0=tb[:, :, 0:64], in1=sinpm[:, tts, 64:128], op=ALU.mult
+            )
+
+        def rope_add(un, half):
+            nc.gpsimd.tensor_tensor(out=stage[(un, half)][:], in0=stage[(un, half)][:], in1=bst[(un, half)][:], op=ALU.add)
+
+        def store(un, part):
+            st, b = divmod(un, 4)
+            width = 1 if un == LASTU else 2
+            rows = slice(NTOK * b, NTOK * (b + 1))
+            h0 = width * part
+            if st < 4:
+                dst = out_0[0, rows, 4 * st + h0 : 4 * st + h0 + width, :]
+            elif st == 4:
+                dst = out_1[0, rows, h0 : h0 + width, :]
+            else:
+                dst = out_2[0, rows, h0 : h0 + width, :]
+            nc.sync.dma_start(
+                out=dst.rearrange("(tt p) h d -> p tt (h d)", p=P),
+                in_=stage[(un, part)][:].rearrange("p tt h d -> p tt (h d)"),
+            )
+
+        for s in range(NG + 1):
+            x = s - RLAG
+            if x >= 0:
+                rotate(x // 4, x % 4, VEC if x % 4 < 2 else ACT)
+                if x // 4 >= 20 and x % 2 == 1:
+                    store(x // 4, (x % 4) // 2)
+            y = s - SLAG
+            if y >= 0 and y % 2 == 0 and y < DIRECT0:
+                silu_pair(y // 2)
+            if s - 2 >= DIRECT0:
+                silu_one(s - 2)
+            if s < NG:
+                project(s)
+            if s == 0:
+                conv_weights()
+            if s == 7:
+                rope_tables()
+            z = s - TLAG
+            if z >= 0 and z % 4 == 0:
+                for hh in range(4):
+                    transposes(z // 4, hh, "tb")
+            if s >= 1:
+                taps(s - 1)
+                conv(s - 1)
+            y = s - PLAG
+            if y >= 0 and y % 2 == 0 and y < DIRECT0:
+                pool_add(y // 2)
+            y = s - ALAG
+            if y >= 0 and y % 2 == 0 and y // 4 < 20:
+                rope_add(y // 4, (y % 4) // 2)
+                store(y // 4, (y % 4) // 2)
+
+        rotate(21, 3, ACT)
+        store(21, 1)
+        for hh in range(4):
+            transposes(22, hh, "tb")
+        for hh in range(3):
+            transposes(23, hh, "u")
+        rotate(22, 0, ACT)
+        rotate(22, 1, ACT)
+        store(22, 0)
+        silu_one(95)
+        transposes(23, 3, "u")
+        rotate(22, 2, VEC)
+        rotate(22, 3, VEC)
+        store(22, 1)
+        rotate(23, 1, ACT)
+        store(23, 1)
+        rotate(23, 0, VEC)
+        store(23, 0)
+        rotate(23, 3, ACT)
+        store(23, 3)
+        rotate(23, 2, VEC)
+        store(23, 2)

@@ -19,7 +19,8 @@ NTOK = 512
 NG = 96
 ACCW = 520
 DIRECT0 = 88
-LASTU = 23
+LASTG = 95
+NWARM = 14
 
 SLAG = 6
 TLAG = 9
@@ -43,7 +44,7 @@ def tile_gpt_pa_kernel(
         for b in range(4):
             t_xc = keep.tile([P, PASSES, 1024], U8, name="xc%d" % b, align_bytes=64)
             t_xp = keep.tile([P, PASSES, 512], U8, name="xp%d" % b, align_bytes=64)
-            t_wcq = keep.tile([P, PASSES, 1024], U8, name="wcq%d" % b, align_bytes=64)
+            t_wcq = keep.tile([P, PASSES, 1024], U8, name="wcq%d" % b, align_bytes=64) if b > 0 else None
             t_wpq = keep.tile([P, PASSES, 512], U8, name="wpq%d" % b, align_bytes=64)
             t_wck = keep.tile([P, PASSES, 512], U8, name="wck%d" % b, align_bytes=64)
             t_wpk = keep.tile([P, PASSES, 256], U8, name="wpk%d" % b, align_bytes=64)
@@ -53,6 +54,9 @@ def tile_gpt_pa_kernel(
             wpq.append(t_wpq)
             wck.append(t_wck)
             wpk.append(t_wpk)
+        wch0 = keep.tile([P, PASSES, 256], U8, name="wch0", align_bytes=64)
+        wcr0 = keep.tile([P, PASSES, 768], U8, name="wcr0", align_bytes=64)
+        zb = keep.tile([P, 512], BF16, name="zb")
         wl = keep.tile([P, 512], BF16, name="wl")
         wd = keep.tile([P, 4, P], F32, name="wd")
         wf = keep.tile([P, 4, 24], F32, name="wf")
@@ -79,6 +83,7 @@ def tile_gpt_pa_kernel(
 
         nc.vector.memset(xp[0][:].bitcast(I32), 0)
         nc.gpsimd.memset(wpq[0][:].bitcast(F32), 0.0)
+        nc.vector.memset(zb[:], 0.0)
         nc.vector.memset(wl[:], 0.0)
         nc.gpsimd.memset(zeros[:], 0.0)
         nc.gpsimd.dma_start(out=wl[0:16, :], in_=q_conv_w.rearrange("(h p) j -> h (p j)", p=P))
@@ -87,21 +92,26 @@ def tile_gpt_pa_kernel(
         make_identity(nc, ident[:])
         nc.scalar.activation(out=scr[:, 0:1], in_=zeros[:, 0:1], func=AF.Silu)
 
+        load_codes(wch0, Wqkv_words, 0, 8, 0, 128)
         load_codes(xc[0], x_words, 0, 4, 0, 512)
-        load_codes(wcq[0], Wqkv_words, 0, 4, 0, 512)
         load_scales(xp[0], x_scales, 0, 512)
         load_scales(wpq[0], Wqkv_scales, 0, 512)
         load_codes(xc[0], x_words, 4, 8, 0, 512)
-        load_codes(wcq[0], Wqkv_words, 4, 8, 0, 512)
+        load_codes(wcr0, Wqkv_words, 0, 8, 128, 512)
+
+        warm = psum.tile([P, NTOK], F32, name="tb", tag="tb", bufs=4)
+        for w in range(NWARM):
+            nc.tensor.matmul(out=warm[:], lhsT=zb[:, 0:P], rhs=zb[:], start=True, stop=True)
 
         for b in range(1, 4):
             nc.vector.memset(xp[b][:].bitcast(I32), 0)
             nc.gpsimd.memset(wpq[b][:].bitcast(F32), 0.0)
         for c in range(4):
             nc.gpsimd.memset(wpk[c][:].bitcast(F32), 0.0)
-        for b in range(1, 4):
-            load_scales(xp[b], x_scales, 512 * b, 512 * (b + 1))
+        load_scales(xp[1], x_scales, 512, 1024)
         load_codes(xc[1], x_words, 0, 8, 512, 1024)
+        load_scales(xp[2], x_scales, 1024, 1536)
+        load_scales(xp[3], x_scales, 1536, 2048)
         nc.sync.dma_start(out=craw[:], in_=cos.rearrange("(t p) i -> p t i", p=P))
         nc.sync.dma_start(out=sraw[:], in_=sin.rearrange("(t p) i -> p t i", p=P))
         load_codes(xc[2], x_words, 0, 8, 1024, 1536)
@@ -134,59 +144,65 @@ def tile_gpt_pa_kernel(
         def info(i):
             st, r = divmod(i, 16)
             b, hh = divmod(r, 4)
+            if st == 0 and hh == 0:
+                return b, wch0, 0, wpq[0], 0, 0
+            if st == 0:
+                return b, wcr0, 128 * (hh - 1), wpq[0], 128 * hh, hh
             if st < 4:
-                return b, wcq[st], wpq[st], 128 * hh, 4 * st + hh
-            return b, wck[hh], wpk[hh], 128 * (st - 4), 16 + 4 * (st - 4) + hh
+                return b, wcq[st], 128 * hh, wpq[st], 128 * hh, 4 * st + hh
+            return b, wck[hh], 128 * (st - 4), wpk[hh], 128 * (st - 4), 16 + 4 * (st - 4) + hh
 
         def pool_tap(i):
-            return i < DIRECT0
+            return i < DIRECT0 and (i // 2) % 4 != 3
 
-        def project(i):
-            b, codes, planes, col, widx = info(i)
-            u = psum.tile([P, NTOK], F32, name="u", tag="u", bufs=4)
-            ubank[i] = u
+        def project(i, lo=0, n=NTOK):
+            b, codes, ccol, planes, pcol, widx = info(i)
+            u = psum.tile([P, n], F32, name="u", tag="u", bufs=4)
+            ubank[(i, lo)] = u
             for g in range(PASSES):
                 nc.tensor.matmul_mx(
                     out=u[:],
-                    lhsT=codes[:, g, 2 * col : 2 * col + 256].bitcast(FP4X4),
-                    lhsT_scale=planes[:, g, col : col + 128],
-                    rhs=xc[b][:, g, :].bitcast(FP4X4),
-                    rhs_scale=xp[b][:, g, :],
+                    lhsT=codes[:, g, 2 * ccol : 2 * ccol + 256].bitcast(FP4X4),
+                    lhsT_scale=planes[:, g, pcol : pcol + 128],
+                    rhs=xc[b][:, g, 2 * lo : 2 * (lo + n)].bitcast(FP4X4),
+                    rhs_scale=xp[b][:, g, lo : lo + n],
                     start=(g == 0),
                     stop=(g == PASSES - 1),
                 )
 
-        def taps(i):
-            b, codes, planes, col, widx = info(i)
+        def taps(i, lo=0, n=NTOK):
+            b, codes, ccol, planes, pcol, widx = info(i)
             pr, e = divmod(i, 2)
-            if e == 0:
+            if e == 0 and lo == 0:
                 a_new = work.tile([P, 2, ACCW], F32, name="acc", tag="acc", bufs=6)
                 acc[pr] = a_new
                 if pool_tap(i):
                     t_new = work.tile([P, 2, NTOK], F32, name="tmp", tag="tmp", bufs=3)
                     tmp[pr] = t_new
             a = acc[pr]
-            u = ubank[i]
-            if b == 0:
+            u = ubank[(i, lo)]
+            if lo == 0 and b == 0:
                 nc.scalar.copy(out=a[:, e, 0:3], in_=zeros[:, 0:3])
-            else:
+            elif lo == 0:
                 nc.scalar.copy(out=a[:, e, 0:3], in_=acc[pr - 2][:, e, NTOK : NTOK + 3])
-            nc.scalar.activation(out=a[:, e, 3 : NTOK + 3], in_=u[:], func=AF.Copy, scale=wf[:, 0, widx : widx + 1])
+            nc.scalar.activation(
+                out=a[:, e, lo + 3 : lo + n + 3], in_=u[:], func=AF.Copy, scale=wf[:, 0, widx : widx + 1]
+            )
             if pool_tap(i):
                 nc.scalar.activation(out=tmp[pr][:, e, :], in_=u[:], func=AF.Copy, scale=wf[:, 3, widx : widx + 1])
 
-        def conv(i):
-            b, codes, planes, col, widx = info(i)
+        def conv(i, lo=0, n=NTOK):
+            b, codes, ccol, planes, pcol, widx = info(i)
             pr, e = divmod(i, 2)
             a = acc[pr]
-            u = ubank[i]
+            u = ubank[(i, lo)]
             for j in (1, 2) if pool_tap(i) else (1, 2, 3):
-                sh = 3 - j
+                sh = lo + 3 - j
                 nc.vector.scalar_tensor_tensor(
-                    out=a[:, e, sh : sh + NTOK],
+                    out=a[:, e, sh : sh + n],
                     in0=u[:],
                     scalar=wf[:, j, widx : widx + 1],
-                    in1=a[:, e, sh : sh + NTOK],
+                    in1=a[:, e, sh : sh + n],
                     op0=ALU.mult,
                     op1=ALU.add,
                 )
@@ -197,20 +213,20 @@ def tile_gpt_pa_kernel(
         def silu_pair(pr):
             nc.scalar.activation(out=acc[pr][:, :, 0:NTOK], in_=acc[pr][:, :, 0:NTOK], func=AF.Silu)
 
-        def silu_one(i):
+        def silu_one(i, lo=0, n=NTOK):
             pr, e = divmod(i, 2)
-            nc.scalar.activation(out=acc[pr][:, e, 0:NTOK], in_=acc[pr][:, e, 0:NTOK], func=AF.Silu)
+            nc.scalar.activation(out=acc[pr][:, e, lo : lo + n], in_=acc[pr][:, e, lo : lo + n], func=AF.Silu)
 
-        def transposes(un, hh, tag):
-            tb = psum.tile([P, 4, P], F32, name=tag, tag=tag, bufs=4)
-            tbank[(un, hh)] = tb
+        def transposes(un, hh, tag, t0=0, t1=4):
+            tb = psum.tile([P, t1 - t0, P], F32, name=tag, tag=tag, bufs=4)
+            tbank[(un, hh, t0)] = tb
             a = acc[2 * un + hh // 2]
-            for tt in range(4):
-                nc.tensor.transpose(out=tb[:, tt, :], in_=a[:, hh % 2, P * tt : P * (tt + 1)], identity=ident[:])
+            for tt in range(t0, t1):
+                nc.tensor.transpose(out=tb[:, tt - t0, :], in_=a[:, hh % 2, P * tt : P * (tt + 1)], identity=ident[:])
 
-        def rotate(un, hh, copy_engine):
+        def rotate(un, hh, copy_engine, t0=0, t1=4):
             b = un % 4
-            width = 1 if un == LASTU else 2
+            width = 1 if un >= 20 else 2
             key, e = (un, hh // width), hh % width
             if key not in stage:
                 s_new = work.tile([P, 4, width, P], F32, name="stage", tag="stage", bufs=6)
@@ -218,12 +234,12 @@ def tile_gpt_pa_kernel(
                 if un < 20:
                     b_new = work.tile([P, 4, width, P], F32, name="bst", tag="bst", bufs=4)
                     bst[key] = b_new
-            tb = tbank[(un, hh)]
+            tb = tbank[(un, hh, t0)]
             if un >= 20:
                 if copy_engine == VEC:
-                    nc.vector.tensor_copy(out=stage[key][:, :, e, :], in_=tb[:])
+                    nc.vector.tensor_copy(out=stage[key][:, t0:t1, e, :], in_=tb[:])
                 else:
-                    nc.scalar.copy(out=stage[key][:, :, e, :], in_=tb[:])
+                    nc.scalar.copy(out=stage[key][:, t0:t1, e, :], in_=tb[:])
                 return
             tts = slice(4 * b, 4 * b + 4)
             nc.vector.tensor_tensor(out=stage[key][:, :, e, :], in0=tb[:], in1=cos2[:, tts, :], op=ALU.mult)
@@ -237,10 +253,10 @@ def tile_gpt_pa_kernel(
         def rope_add(un, half):
             nc.gpsimd.tensor_tensor(out=stage[(un, half)][:], in0=stage[(un, half)][:], in1=bst[(un, half)][:], op=ALU.add)
 
-        def store(un, part):
+        def store(un, part, t0=0, t1=4):
             st, b = divmod(un, 4)
-            width = 1 if un == LASTU else 2
-            rows = slice(NTOK * b, NTOK * (b + 1))
+            width = 1 if un >= 20 else 2
+            rows = slice(NTOK * b + P * t0, NTOK * b + P * t1)
             h0 = width * part
             if st < 4:
                 dst = out_0[0, rows, 4 * st + h0 : 4 * st + h0 + width, :]
@@ -250,60 +266,69 @@ def tile_gpt_pa_kernel(
                 dst = out_2[0, rows, h0 : h0 + width, :]
             nc.sync.dma_start(
                 out=dst.rearrange("(tt p) h d -> p tt (h d)", p=P),
-                in_=stage[(un, part)][:].rearrange("p tt h d -> p tt (h d)"),
+                in_=stage[(un, part)][:, t0:t1, :, :].rearrange("p tt h d -> p tt (h d)"),
             )
 
-        for s in range(NG + 1):
+        for s in range(NG):
             x = s - RLAG
+            if 0 <= x < 80:
+                rotate(x // 4, x % 4, VEC)
+            x = s - 90
             if x >= 0:
-                rotate(x // 4, x % 4, VEC if x % 4 < 2 else ACT)
-                if x // 4 >= 20 and x % 2 == 1:
-                    store(x // 4, (x % 4) // 2)
+                for hh in (2 * (x % 2), 2 * (x % 2) + 1):
+                    rotate(20 + x // 2, hh, VEC if hh % 2 == 0 else ACT)
+                    store(20 + x // 2, hh)
             y = s - SLAG
-            if y >= 0 and y % 2 == 0 and y < DIRECT0:
+            if y >= 0 and y % 2 == 0 and y // 2 < 43:
                 silu_pair(y // 2)
-            if s - 2 >= DIRECT0:
-                silu_one(s - 2)
-            if s < NG:
+            if s == 91:
+                silu_pair(43)
+            if s < LASTG:
                 project(s)
+            else:
+                project(s, 0, 256)
+                project(s, 256, 256)
             if s == 0:
                 conv_weights()
             if s == 7:
                 rope_tables()
-            z = s - TLAG
-            if z >= 0 and z % 4 == 0:
-                for hh in range(4):
-                    transposes(z // 4, hh, "tb")
             if s >= 1:
                 taps(s - 1)
+            if s - 2 >= DIRECT0:
+                silu_one(s - 2)
+            z = s - TLAG
+            if (z >= 0 and z % 4 == 0 and z // 4 <= 20) or s in (91, 93):
+                for hh in range(4):
+                    transposes(z // 4 if s < 90 else 20 + (s - 89) // 2, hh, "tb")
+            if s >= 1:
                 conv(s - 1)
             y = s - PLAG
-            if y >= 0 and y % 2 == 0 and y < DIRECT0:
+            if y >= 0 and y % 2 == 0 and pool_tap(y):
                 pool_add(y // 2)
             y = s - ALAG
             if y >= 0 and y % 2 == 0 and y // 4 < 20:
                 rope_add(y // 4, (y % 4) // 2)
                 store(y // 4, (y % 4) // 2)
 
-        rotate(21, 3, ACT)
-        store(21, 1)
-        for hh in range(4):
-            transposes(22, hh, "tb")
-        for hh in range(3):
-            transposes(23, hh, "u")
-        rotate(22, 0, ACT)
-        rotate(22, 1, ACT)
-        store(22, 0)
-        silu_one(95)
-        transposes(23, 3, "u")
-        rotate(22, 2, VEC)
-        rotate(22, 3, VEC)
-        store(22, 1)
-        rotate(23, 1, ACT)
-        store(23, 1)
-        rotate(23, 0, VEC)
+        taps(LASTG, 0, 256)
+        conv(LASTG, 0, 256)
+        taps(LASTG, 256, 256)
+        conv(LASTG, 256, 256)
+        transposes(23, 0, "tb")
+        transposes(23, 1, "tb")
+        silu_one(94)
+        transposes(23, 2, "tb")
+        rotate(23, 0, ACT)
         store(23, 0)
-        rotate(23, 3, ACT)
-        store(23, 3)
+        silu_one(LASTG, 0, 256)
+        transposes(23, 3, "tb", 0, 2)
+        silu_one(LASTG, 256, 256)
+        transposes(23, 3, "u", 2, 4)
+        rotate(23, 1, VEC)
+        store(23, 1)
         rotate(23, 2, VEC)
         store(23, 2)
+        rotate(23, 3, ACT, 0, 2)
+        store(23, 3, 0, 2)
+        rotate(23, 3, ACT, 2, 4)
+        store(23, 3, 2, 4)

@@ -18,7 +18,8 @@ PASSES = 8
 NTOK = 512
 NG = 96
 ACCW = 520
-DIRECT0 = 88
+DIRECT0 = 94
+SINGLE0 = 80
 LASTG = 95
 NWARM = 14
 
@@ -62,8 +63,8 @@ def tile_gpt_pa_kernel(
         wf = keep.tile([P, 4, 24], F32, name="wf")
         craw = keep.tile([P, 16, 64], BF16, name="craw")
         sraw = keep.tile([P, 16, 64], BF16, name="sraw")
-        cos2 = keep.tile([P, 16, 128], F32, name="cos2")
-        sinpm = keep.tile([P, 16, 128], F32, name="sinpm")
+        cs1 = keep.tile([P, 16, 128], F32, name="cs1")
+        cs2 = keep.tile([P, 16, 128], F32, name="cs2")
         ident = keep.tile([P, P], F32, name="ident")
         zeros = keep.tile([P, 8], F32, name="zeros")
         scr = keep.tile([P, 8], F32, name="scr")
@@ -134,10 +135,10 @@ def tile_gpt_pa_kernel(
             nc.vector.tensor_copy(out=wf[:], in_=wt[:, :, 0:24])
 
         def rope_tables():
-            nc.scalar.copy(out=cos2[:, :, 0:64], in_=craw[:])
-            nc.scalar.copy(out=cos2[:, :, 64:128], in_=craw[:])
-            nc.vector.tensor_scalar_mul(out=sinpm[:, :, 0:64], in0=sraw[:], scalar1=-1.0)
-            nc.vector.tensor_copy(out=sinpm[:, :, 64:128], in_=sraw[:])
+            nc.scalar.copy(out=cs1[:, :, 0:64], in_=craw[:])
+            nc.scalar.copy(out=cs1[:, :, 64:128], in_=sraw[:])
+            nc.vector.tensor_scalar_mul(out=cs2[:, :, 0:64], in0=sraw[:], scalar1=-1.0)
+            nc.vector.tensor_copy(out=cs2[:, :, 64:128], in_=craw[:])
 
         ubank, acc, tmp, tbank, stage, bst = {}, {}, {}, {}, {}, {}
 
@@ -153,7 +154,7 @@ def tile_gpt_pa_kernel(
             return b, wck[hh], 128 * (st - 4), wpk[hh], 128 * (st - 4), 16 + 4 * (st - 4) + hh
 
         def pool_tap(i):
-            return i < DIRECT0 and (i // 2) % 4 != 3
+            return i < 88 or 92 <= i < DIRECT0
 
         def project(i, lo=0, n=NTOK):
             b, codes, ccol, planes, pcol, widx = info(i)
@@ -191,24 +192,26 @@ def tile_gpt_pa_kernel(
             if pool_tap(i):
                 nc.scalar.activation(out=tmp[pr][:, e, :], in_=u[:], func=AF.Copy, scale=wf[:, 3, widx : widx + 1])
 
-        def conv(i, lo=0, n=NTOK):
+        def tap(i, j, lo=0, n=NTOK):
             b, codes, ccol, planes, pcol, widx = info(i)
             pr, e = divmod(i, 2)
             a = acc[pr]
-            u = ubank[(i, lo)]
-            for j in (1, 2) if pool_tap(i) else (1, 2, 3):
-                sh = lo + 3 - j
-                nc.vector.scalar_tensor_tensor(
-                    out=a[:, e, sh : sh + n],
-                    in0=u[:],
-                    scalar=wf[:, j, widx : widx + 1],
-                    in1=a[:, e, sh : sh + n],
-                    op0=ALU.mult,
-                    op1=ALU.add,
-                )
+            sh = lo + 3 - j
+            nc.vector.scalar_tensor_tensor(
+                out=a[:, e, sh : sh + n],
+                in0=ubank[(i, lo)][:],
+                scalar=wf[:, j, widx : widx + 1],
+                in1=a[:, e, sh : sh + n],
+                op0=ALU.mult,
+                op1=ALU.add,
+            )
 
         def pool_add(pr):
             nc.gpsimd.tensor_tensor(out=acc[pr][:, :, 0:NTOK], in0=acc[pr][:, :, 0:NTOK], in1=tmp[pr][:], op=ALU.add)
+
+        def pool_add_one(i):
+            pr, e = divmod(i, 2)
+            nc.gpsimd.tensor_tensor(out=acc[pr][:, e, 0:NTOK], in0=acc[pr][:, e, 0:NTOK], in1=tmp[pr][:, e, :], op=ALU.add)
 
         def silu_pair(pr):
             nc.scalar.activation(out=acc[pr][:, :, 0:NTOK], in_=acc[pr][:, :, 0:NTOK], func=AF.Silu)
@@ -224,31 +227,33 @@ def tile_gpt_pa_kernel(
             for tt in range(t0, t1):
                 nc.tensor.transpose(out=tb[:, tt - t0, :], in_=a[:, hh % 2, P * tt : P * (tt + 1)], identity=ident[:])
 
-        def rotate(un, hh, copy_engine, t0=0, t1=4):
+        def rotate(un, hh, half):
+            key, e = (un, hh // 2), hh % 2
+            if key not in stage:
+                s_new = work.tile([P, 4, 2, P], F32, name="stage", tag="stage", bufs=6)
+                stage[key] = s_new
+                b_new = work.tile([P, 4, 2, P], F32, name="bst", tag="bst", bufs=4)
+                bst[key] = b_new
+            tts = slice(4 * (un % 4), 4 * (un % 4) + 4)
+            nc.vector.tensor_tensor(
+                out=(bst if half else stage)[key][:, :, e, :].rearrange("p t (r i) -> p t r i", r=2),
+                in0=tbank[(un, hh, 0)][:, :, 64 * half : 64 * half + 64].unsqueeze(2).to_broadcast([P, 4, 2, 64]),
+                in1=(cs2 if half else cs1)[:, tts, :].rearrange("p t (r i) -> p t r i", r=2),
+                op=ALU.mult,
+            )
+
+        def copy_out(un, hh, copy_engine, t0=0, t1=4):
             b = un % 4
             width = 1 if un >= 20 else 2
             key, e = (un, hh // width), hh % width
             if key not in stage:
                 s_new = work.tile([P, 4, width, P], F32, name="stage", tag="stage", bufs=6)
                 stage[key] = s_new
-                if un < 20:
-                    b_new = work.tile([P, 4, width, P], F32, name="bst", tag="bst", bufs=4)
-                    bst[key] = b_new
             tb = tbank[(un, hh, t0)]
-            if un >= 20:
-                if copy_engine == VEC:
-                    nc.vector.tensor_copy(out=stage[key][:, t0:t1, e, :], in_=tb[:])
-                else:
-                    nc.scalar.copy(out=stage[key][:, t0:t1, e, :], in_=tb[:])
-                return
-            tts = slice(4 * b, 4 * b + 4)
-            nc.vector.tensor_tensor(out=stage[key][:, :, e, :], in0=tb[:], in1=cos2[:, tts, :], op=ALU.mult)
-            nc.vector.tensor_tensor(
-                out=bst[key][:, :, e, 0:64], in0=tb[:, :, 64:128], in1=sinpm[:, tts, 0:64], op=ALU.mult
-            )
-            nc.vector.tensor_tensor(
-                out=bst[key][:, :, e, 64:128], in0=tb[:, :, 0:64], in1=sinpm[:, tts, 64:128], op=ALU.mult
-            )
+            if copy_engine == VEC:
+                nc.vector.tensor_copy(out=stage[key][:, t0:t1, e, :], in_=tb[:])
+            else:
+                nc.scalar.copy(out=stage[key][:, t0:t1, e, :], in_=tb[:])
 
         def rope_add(un, half):
             nc.gpsimd.tensor_tensor(out=stage[(un, half)][:], in0=stage[(un, half)][:], in1=bst[(un, half)][:], op=ALU.add)
@@ -269,20 +274,35 @@ def tile_gpt_pa_kernel(
                 in_=stage[(un, part)][:, t0:t1, :, :].rearrange("p tt h d -> p tt (h d)"),
             )
 
-        for s in range(NG):
+        t_step = {89: 20, 91: 21, 93: 22}
+        for un in range(20):
+            t_step[4 * un + TLAG] = un
+        c_step = {}
+        for s0, un in ((89, 20), (91, 21), (93, 22)):
+            c_step[s0 + 1] = (un, 0)
+            c_step[s0 + 2] = (un, 2)
+
+        def vector_step(s):
+            i = s - 1
             x = s - RLAG
             if 0 <= x < 80:
-                rotate(x // 4, x % 4, VEC)
-            x = s - 90
-            if x >= 0:
-                for hh in (2 * (x % 2), 2 * (x % 2) + 1):
-                    rotate(20 + x // 2, hh, VEC if hh % 2 == 0 else ACT)
-                    store(20 + x // 2, hh)
+                rotate(x // 4, x % 4, 0)
+            if 0 <= i < LASTG:
+                tap(i, 1)
+            if 0 <= x < 80:
+                rotate(x // 4, x % 4, 1)
+            if s in c_step:
+                copy_out(c_step[s][0], c_step[s][1], VEC)
+                store(c_step[s][0], c_step[s][1])
+            if 0 <= i < LASTG - 1:
+                tap(i, 2)
+                if not pool_tap(i):
+                    tap(i, 3)
+
+        for s in range(NG):
             y = s - SLAG
-            if y >= 0 and y % 2 == 0 and y // 2 < 43:
+            if y >= 0 and y % 2 == 0 and y < SINGLE0:
                 silu_pair(y // 2)
-            if s == 91:
-                silu_pair(43)
             if s < LASTG:
                 project(s)
             else:
@@ -294,41 +314,52 @@ def tile_gpt_pa_kernel(
                 rope_tables()
             if s >= 1:
                 taps(s - 1)
-            if s - 2 >= DIRECT0:
+            if SINGLE0 <= s - 3 and pool_tap(s - 3):
+                silu_one(s - 3)
+            if SINGLE0 <= s - 2 and not pool_tap(s - 2):
                 silu_one(s - 2)
-            z = s - TLAG
-            if (z >= 0 and z % 4 == 0 and z // 4 <= 20) or s in (91, 93):
+            if s in c_step:
+                copy_out(c_step[s][0], c_step[s][1] + 1, ACT)
+                store(c_step[s][0], c_step[s][1] + 1)
+            vector_step(s)
+            if s in t_step:
                 for hh in range(4):
-                    transposes(z // 4 if s < 90 else 20 + (s - 89) // 2, hh, "tb")
-            if s >= 1:
-                conv(s - 1)
+                    transposes(t_step[s], hh, "tb")
             y = s - PLAG
-            if y >= 0 and y % 2 == 0 and pool_tap(y):
+            if y >= 0 and y % 2 == 0 and y < SINGLE0:
                 pool_add(y // 2)
+            if SINGLE0 <= s - 2 and pool_tap(s - 2):
+                pool_add_one(s - 2)
             y = s - ALAG
             if y >= 0 and y % 2 == 0 and y // 4 < 20:
                 rope_add(y // 4, (y % 4) // 2)
                 store(y // 4, (y % 4) // 2)
 
         taps(LASTG, 0, 256)
-        conv(LASTG, 0, 256)
+        tap(LASTG - 1, 2)
+        tap(LASTG, 1, 0, 256)
+        tap(LASTG - 1, 3)
+        silu_one(93)
         taps(LASTG, 256, 256)
-        conv(LASTG, 256, 256)
-        transposes(23, 0, "tb")
-        transposes(23, 1, "tb")
         silu_one(94)
-        transposes(23, 2, "tb")
-        rotate(23, 0, ACT)
+        tap(LASTG, 2, 0, 256)
+        tap(LASTG, 1, 256, 256)
+        tap(LASTG, 3, 0, 256)
+        tap(LASTG, 2, 256, 256)
+        tap(LASTG, 3, 256, 256)
+        for hh in range(3):
+            transposes(23, hh, "tb")
+        copy_out(23, 0, ACT)
         store(23, 0)
         silu_one(LASTG, 0, 256)
         transposes(23, 3, "tb", 0, 2)
+        copy_out(23, 1, ACT)
+        store(23, 1)
         silu_one(LASTG, 256, 256)
         transposes(23, 3, "u", 2, 4)
-        rotate(23, 1, VEC)
-        store(23, 1)
-        rotate(23, 2, VEC)
+        copy_out(23, 2, VEC)
         store(23, 2)
-        rotate(23, 3, ACT, 0, 2)
+        copy_out(23, 3, VEC, 0, 2)
         store(23, 3, 0, 2)
-        rotate(23, 3, ACT, 2, 4)
+        copy_out(23, 3, ACT, 2, 4)
         store(23, 3, 2, 4)

@@ -100,7 +100,7 @@ def tile_gpt_pa_kernel(
         load_codes(xc[0], x_words, 4, 8, 0, 512)
         load_codes(wcr0, Wqkv_words, 0, 8, 128, 512)
 
-        warm = psum.tile([P, NTOK], F32, name="tb", tag="tb", bufs=4)
+        warm = psum.tile([P, NTOK], F32, name="tb", tag="tb", bufs=5)
         for w in range(NWARM):
             nc.tensor.matmul(out=warm[:], lhsT=zb[:, 0:P], rhs=zb[:], start=True, stop=True)
 
@@ -129,7 +129,7 @@ def tile_gpt_pa_kernel(
         nc.vector.tensor_copy(out=wd[:], in_=wl[:].rearrange("h (p j) -> h j p", j=4))
 
         def conv_weights():
-            wt = psum.tile([P, 4, P], F32, name="tb", tag="tb", bufs=4)
+            wt = psum.tile([P, 4, P], F32, name="tb", tag="tb", bufs=5)
             for j in range(4):
                 nc.tensor.transpose(out=wt[:, j, :], in_=wd[:, j, :], identity=ident[:])
             nc.vector.tensor_copy(out=wf[:], in_=wt[:, :, 0:24])
@@ -158,7 +158,7 @@ def tile_gpt_pa_kernel(
 
         def project(i, lo=0, n=NTOK):
             b, codes, ccol, planes, pcol, widx = info(i)
-            u = psum.tile([P, n], F32, name="u", tag="u", bufs=4)
+            u = psum.tile([P, n], F32, name="u", tag="u", bufs=3)
             ubank[(i, lo)] = u
             for g in range(PASSES):
                 nc.tensor.matmul_mx(
@@ -221,7 +221,7 @@ def tile_gpt_pa_kernel(
             nc.scalar.activation(out=acc[pr][:, e, lo : lo + n], in_=acc[pr][:, e, lo : lo + n], func=AF.Silu)
 
         def transposes(un, hh, tag, t0=0, t1=4):
-            tb = psum.tile([P, t1 - t0, P], F32, name=tag, tag=tag, bufs=4)
+            tb = psum.tile([P, t1 - t0, P], F32, name=tag, tag=tag, bufs=(3 if tag == "u" else 5))
             tbank[(un, hh, t0)] = tb
             a = acc[2 * un + hh // 2]
             for tt in range(t0, t1):
@@ -291,7 +291,7 @@ def tile_gpt_pa_kernel(
                 tap(i, 1)
             if 0 <= x < 80:
                 rotate(x // 4, x % 4, 1)
-            if s in c_step:
+            if s in c_step and not (c_step[s][1] == 2):
                 copy_out(c_step[s][0], c_step[s][1], VEC)
                 store(c_step[s][0], c_step[s][1])
             if 0 <= i < LASTG - 1:
@@ -312,13 +312,17 @@ def tile_gpt_pa_kernel(
                 conv_weights()
             if s == 7:
                 rope_tables()
+            if s in c_step and c_step[s][1] == 2:
+                for hh in (2, 3):
+                    copy_out(c_step[s][0], hh, ACT)
+                    store(c_step[s][0], hh)
             if s >= 1:
                 taps(s - 1)
             if SINGLE0 <= s - 3 and pool_tap(s - 3):
                 silu_one(s - 3)
             if SINGLE0 <= s - 2 and not pool_tap(s - 2):
                 silu_one(s - 2)
-            if s in c_step:
+            if s in c_step and not (c_step[s][1] == 2):
                 copy_out(c_step[s][0], c_step[s][1] + 1, ACT)
                 store(c_step[s][0], c_step[s][1] + 1)
             vector_step(s)

@@ -28,7 +28,7 @@ TLAG = 9
 RLAG = 10
 PLAG = 3
 ALAG = 12
-VEC, ACT = 0, 1
+PERM0 = 20
 
 
 def tile_gpt_pa_kernel(
@@ -57,6 +57,8 @@ def tile_gpt_pa_kernel(
             wpk.append(t_wpk)
         wch0 = keep.tile([P, PASSES, 256], U8, name="wch0", align_bytes=64)
         wcr0 = keep.tile([P, PASSES, 768], U8, name="wcr0", align_bytes=64)
+        wcv = keep.tile([P, PASSES, 1024], U8, name="wcv", align_bytes=64)
+        wpv = keep.tile([P, PASSES, 512], U8, name="wpv", align_bytes=64)
         zb = keep.tile([P, 512], BF16, name="zb")
         wl = keep.tile([P, 512], BF16, name="wl")
         wd = keep.tile([P, 4, P], F32, name="wd")
@@ -89,7 +91,10 @@ def tile_gpt_pa_kernel(
         nc.gpsimd.memset(zeros[:], 0.0)
         nc.gpsimd.dma_start(out=wl[0:16, :], in_=q_conv_w.rearrange("(h p) j -> h (p j)", p=P))
         nc.gpsimd.dma_start(out=wl[16:20, :], in_=k_conv_w.rearrange("(h p) j -> h (p j)", p=P))
-        nc.gpsimd.dma_start(out=wl[20:24, :], in_=v_conv_w.rearrange("(h p) j -> h (p j)", p=P))
+        nc.gpsimd.dma_start(
+            out=wl[20:24, :].rearrange("m (a x) -> m a x", a=4),
+            in_=v_conv_w.rearrange("(a m r) j -> m a (r j)", a=4, m=4),
+        )
         make_identity(nc, ident[:])
         nc.scalar.activation(out=scr[:, 0:1], in_=zeros[:, 0:1], func=AF.Silu)
 
@@ -134,13 +139,26 @@ def tile_gpt_pa_kernel(
                 nc.tensor.transpose(out=wt[:, j, :], in_=wd[:, j, :], identity=ident[:])
             nc.vector.tensor_copy(out=wf[:], in_=wt[:, :, 0:24])
 
+        def permute_value_weights(k):
+            a = k % 4
+            if k < 4:
+                nc.vector.tensor_copy(
+                    out=wcv[:].bitcast(I32).rearrange("p g (m a w) -> p g m a w", m=4, a=4)[:, :, :, a, :],
+                    in_=wck[a][:, :, 256:512].bitcast(I32).rearrange("p g (m w) -> p g m w", m=4),
+                )
+            else:
+                nc.vector.tensor_copy(
+                    out=wpv[:].bitcast(I32).rearrange("p g (m a w) -> p g m a w", m=4, a=4)[:, :, :, a, :],
+                    in_=wpk[a][:, :, 128:256].bitcast(I32).rearrange("p g (m w) -> p g m w", m=4),
+                )
+
         def rope_tables():
             nc.scalar.copy(out=cs1[:, :, 0:64], in_=craw[:])
             nc.scalar.copy(out=cs1[:, :, 64:128], in_=sraw[:])
             nc.vector.tensor_scalar_mul(out=cs2[:, :, 0:64], in0=sraw[:], scalar1=-1.0)
             nc.vector.tensor_copy(out=cs2[:, :, 64:128], in_=craw[:])
 
-        ubank, acc, tmp, tbank, stage, bst = {}, {}, {}, {}, {}, {}
+        ubank, acc, tmp, tbank, stage, bst, vin, vout = {}, {}, {}, {}, {}, {}, {}, {}
 
         def info(i):
             st, r = divmod(i, 16)
@@ -151,7 +169,9 @@ def tile_gpt_pa_kernel(
                 return b, wcr0, 128 * (hh - 1), wpq[0], 128 * hh, hh
             if st < 4:
                 return b, wcq[st], 128 * hh, wpq[st], 128 * hh, 4 * st + hh
-            return b, wck[hh], 128 * (st - 4), wpk[hh], 128 * (st - 4), 16 + 4 * (st - 4) + hh
+            if st == 4:
+                return b, wck[hh], 0, wpk[hh], 0, 16 + hh
+            return b, wcv, 128 * hh, wpv, 128 * hh, 20 + hh
 
         def pool_tap(i):
             return i < 88 or 92 <= i < DIRECT0
@@ -216,9 +236,31 @@ def tile_gpt_pa_kernel(
         def silu_pair(pr):
             nc.scalar.activation(out=acc[pr][:, :, 0:NTOK], in_=acc[pr][:, :, 0:NTOK], func=AF.Silu)
 
-        def silu_one(i, lo=0, n=NTOK):
+        def silu_value(i, halves=(0, 1)):
             pr, e = divmod(i, 2)
-            nc.scalar.activation(out=acc[pr][:, e, lo : lo + n], in_=acc[pr][:, e, lo : lo + n], func=AF.Silu)
+            b, m = divmod(i - SINGLE0, 4)
+            for hf in halves:
+                if (b, hf) not in vin:
+                    v_new = work.tile([P, 8, 4, 32], F32, name="stage", tag="stage", bufs=6, align_bytes=64)
+                    vin[(b, hf)] = v_new
+                nc.scalar.activation(
+                    out=vin[(b, hf)][:, :, m, :],
+                    in_=acc[pr][:, e, 256 * hf : 256 * hf + 256].rearrange("p (k c) -> p k c", c=32),
+                    func=AF.Silu,
+                )
+
+        def turn_value(b, hf):
+            o_new = work.tile([P, 8, 4, 32], F32, name="bst", tag="bst", bufs=4, align_bytes=64)
+            vout[(b, hf)] = o_new
+            nc.vector.transpose(
+                out=o_new[:].rearrange("p k m r -> p (k m r)"), in_=vin[(b, hf)][:].rearrange("p k m c -> p (k m c)")
+            )
+            r0 = NTOK * b + 256 * hf
+            for a in range(4):
+                nc.sync.dma_start(
+                    out=out_2[0, r0 : r0 + 256, a, :].rearrange("(k c) d -> c k d", c=32),
+                    in_=o_new[32 * a : 32 * a + 32, :, :, :].rearrange("c k m r -> c k (m r)"),
+                )
 
         def transposes(un, hh, tag, t0=0, t1=4):
             tb = psum.tile([P, t1 - t0, P], F32, name=tag, tag=tag, bufs=(3 if tag == "u" else 5))
@@ -230,9 +272,9 @@ def tile_gpt_pa_kernel(
         def rotate(un, hh, half):
             key, e = (un, hh // 2), hh % 2
             if key not in stage:
-                s_new = work.tile([P, 4, 2, P], F32, name="stage", tag="stage", bufs=6)
+                s_new = work.tile([P, 4, 2, P], F32, name="stage", tag="stage", bufs=6, align_bytes=64)
                 stage[key] = s_new
-                b_new = work.tile([P, 4, 2, P], F32, name="bst", tag="bst", bufs=4)
+                b_new = work.tile([P, 4, 2, P], F32, name="bst", tag="bst", bufs=4, align_bytes=64)
                 bst[key] = b_new
             tts = slice(4 * (un % 4), 4 * (un % 4) + 4)
             nc.vector.tensor_tensor(
@@ -241,19 +283,6 @@ def tile_gpt_pa_kernel(
                 in1=(cs2 if half else cs1)[:, tts, :].rearrange("p t (r i) -> p t r i", r=2),
                 op=ALU.mult,
             )
-
-        def copy_out(un, hh, copy_engine, t0=0, t1=4):
-            b = un % 4
-            width = 1 if un >= 20 else 2
-            key, e = (un, hh // width), hh % width
-            if key not in stage:
-                s_new = work.tile([P, 4, width, P], F32, name="stage", tag="stage", bufs=6)
-                stage[key] = s_new
-            tb = tbank[(un, hh, t0)]
-            if copy_engine == VEC:
-                nc.vector.tensor_copy(out=stage[key][:, t0:t1, e, :], in_=tb[:])
-            else:
-                nc.scalar.copy(out=stage[key][:, t0:t1, e, :], in_=tb[:])
 
         def rope_add(un, half):
             nc.gpsimd.tensor_tensor(out=stage[(un, half)][:], in0=stage[(un, half)][:], in1=bst[(un, half)][:], op=ALU.add)
@@ -274,30 +303,30 @@ def tile_gpt_pa_kernel(
                 in_=stage[(un, part)][:, t0:t1, :, :].rearrange("p tt h d -> p tt (h d)"),
             )
 
-        t_step = {89: 20, 91: 21, 93: 22}
+        t_step = {}
         for un in range(20):
             t_step[4 * un + TLAG] = un
-        c_step = {}
-        for s0, un in ((89, 20), (91, 21), (93, 22)):
-            c_step[s0 + 1] = (un, 0)
-            c_step[s0 + 2] = (un, 2)
+        v_step = {87: 0, 91: 1, 94: 2}
 
         def vector_step(s):
             i = s - 1
             x = s - RLAG
+            if PERM0 <= s < PERM0 + 8:
+                permute_value_weights(s - PERM0)
             if 0 <= x < 80:
                 rotate(x // 4, x % 4, 0)
             if 0 <= i < LASTG:
                 tap(i, 1)
             if 0 <= x < 80:
                 rotate(x // 4, x % 4, 1)
-            if s in c_step and not (c_step[s][1] == 2):
-                copy_out(c_step[s][0], c_step[s][1], VEC)
-                store(c_step[s][0], c_step[s][1])
+            if s in v_step:
+                turn_value(v_step[s], 0)
             if 0 <= i < LASTG - 1:
                 tap(i, 2)
                 if not pool_tap(i):
                     tap(i, 3)
+            if s in v_step:
+                turn_value(v_step[s], 1)
 
         for s in range(NG):
             y = s - SLAG
@@ -312,19 +341,12 @@ def tile_gpt_pa_kernel(
                 conv_weights()
             if s == 7:
                 rope_tables()
-            if s in c_step and c_step[s][1] == 2:
-                for hh in (2, 3):
-                    copy_out(c_step[s][0], hh, ACT)
-                    store(c_step[s][0], hh)
             if s >= 1:
                 taps(s - 1)
             if SINGLE0 <= s - 3 and pool_tap(s - 3):
-                silu_one(s - 3)
+                silu_value(s - 3)
             if SINGLE0 <= s - 2 and not pool_tap(s - 2):
-                silu_one(s - 2)
-            if s in c_step and not (c_step[s][1] == 2):
-                copy_out(c_step[s][0], c_step[s][1] + 1, ACT)
-                store(c_step[s][0], c_step[s][1] + 1)
+                silu_value(s - 2)
             vector_step(s)
             if s in t_step:
                 for hh in range(4):
@@ -343,27 +365,15 @@ def tile_gpt_pa_kernel(
         tap(LASTG - 1, 2)
         tap(LASTG, 1, 0, 256)
         tap(LASTG - 1, 3)
-        silu_one(93)
+        silu_value(93)
         taps(LASTG, 256, 256)
-        silu_one(94)
+        silu_value(94)
         tap(LASTG, 2, 0, 256)
         tap(LASTG, 1, 256, 256)
         tap(LASTG, 3, 0, 256)
         tap(LASTG, 2, 256, 256)
+        silu_value(LASTG, (0,))
         tap(LASTG, 3, 256, 256)
-        for hh in range(3):
-            transposes(23, hh, "tb")
-        copy_out(23, 0, ACT)
-        store(23, 0)
-        silu_one(LASTG, 0, 256)
-        transposes(23, 3, "tb", 0, 2)
-        copy_out(23, 1, ACT)
-        store(23, 1)
-        silu_one(LASTG, 256, 256)
-        transposes(23, 3, "u", 2, 4)
-        copy_out(23, 2, VEC)
-        store(23, 2)
-        copy_out(23, 3, VEC, 0, 2)
-        store(23, 3, 0, 2)
-        copy_out(23, 3, ACT, 2, 4)
-        store(23, 3, 2, 4)
+        turn_value(3, 0)
+        silu_value(LASTG, (1,))
+        turn_value(3, 1)

@@ -28,7 +28,8 @@ TLAG = 9
 RLAG = 10
 PLAG = 3
 ALAG = 12
-PERM0 = 20
+PERM0 = 22
+VLAG = 5
 
 
 def tile_gpt_pa_kernel(
@@ -158,7 +159,7 @@ def tile_gpt_pa_kernel(
             nc.vector.tensor_scalar_mul(out=cs2[:, :, 0:64], in0=sraw[:], scalar1=-1.0)
             nc.vector.tensor_copy(out=cs2[:, :, 64:128], in_=craw[:])
 
-        ubank, acc, tmp, tbank, stage, bst, vin, vout = {}, {}, {}, {}, {}, {}, {}, {}
+        ubank, acc, tmp, tbank, stage, bst, vin, vout, vrow = {}, {}, {}, {}, {}, {}, {}, {}, {}
 
         def info(i):
             st, r = divmod(i, 16)
@@ -174,7 +175,7 @@ def tile_gpt_pa_kernel(
             return b, wcv, 128 * hh, wpv, 128 * hh, 20 + hh
 
         def pool_tap(i):
-            return i < 88 or 92 <= i < DIRECT0
+            return i < 90 or 92 <= i < DIRECT0
 
         def project(i, lo=0, n=NTOK):
             b, codes, ccol, planes, pcol, widx = info(i)
@@ -262,6 +263,44 @@ def tile_gpt_pa_kernel(
                     in_=o_new[32 * a : 32 * a + 32, :, :, :].rearrange("c k m r -> c k (m r)"),
                 )
 
+        def empty_value(b, m):
+            for half in (0, 1):
+                if (b, half) not in vrow:
+                    r_new = work.tile([P, 2, 4, 4, 32], F32, name="stage", tag="stage", bufs=6, align_bytes=64)
+                    vrow[(b, half)] = r_new
+                nc.scalar.activation(
+                    out=vrow[(b, half)][:, :, :, m, :],
+                    in_=tbank[(20 + b, m, 0)][:, 2 * half : 2 * half + 2, :].rearrange("p t (a r) -> p t a r", a=4),
+                    func=AF.Silu,
+                )
+
+        def empty_last(m, halves=(0, 1)):
+            for half in halves:
+                if (3, half) not in vrow:
+                    r_new = work.tile([P, 2, 4, 4, 32], F32, name="stage", tag="stage", bufs=6, align_bytes=64)
+                    vrow[(3, half)] = r_new
+                if m < 3:
+                    src = tbank[(23, m, 0)][:, 2 * half : 2 * half + 2, :]
+                else:
+                    src = tbank[(23, m, 2 * half)][:]
+                nc.scalar.activation(
+                    out=vrow[(3, half)][:, :, :, m, :], in_=src.rearrange("p t (a r) -> p t a r", a=4), func=AF.Silu
+                )
+
+        def store_rows(b, half, t0=0, t1=2):
+            r0 = NTOK * b + 256 * half
+            nc.sync.dma_start(
+                out=out_2[0, r0 + P * t0 : r0 + P * t1, :, :].rearrange("(t p) a d -> p t (a d)", p=P),
+                in_=vrow[(b, half)][:, t0:t1, :, :, :].rearrange("p t a m r -> p t (a m r)"),
+            )
+
+        def empty_tile(half, tt):
+            nc.scalar.activation(
+                out=vrow[(3, half)][:, tt : tt + 1, :, 3, :],
+                in_=tbank[(23, 3, 2 * half)][:, tt : tt + 1, :].rearrange("p t (a r) -> p t a r", a=4),
+                func=AF.Silu,
+            )
+
         def transposes(un, hh, tag, t0=0, t1=4):
             tb = psum.tile([P, t1 - t0, P], F32, name=tag, tag=tag, bufs=(3 if tag == "u" else 5))
             tbank[(un, hh, t0)] = tb
@@ -303,16 +342,16 @@ def tile_gpt_pa_kernel(
                 in_=stage[(un, part)][:, t0:t1, :, :].rearrange("p tt h d -> p tt (h d)"),
             )
 
-        t_step = {}
+        t_step = {93: 22}
         for un in range(20):
             t_step[4 * un + TLAG] = un
-        v_step = {87: 0, 91: 1, 94: 2}
+        v_step = {90: (0, 0), 91: (0, 1), 93: (1, 0), 94: (1, 1)}
 
         def vector_step(s):
             i = s - 1
             x = s - RLAG
-            if PERM0 <= s < PERM0 + 8:
-                permute_value_weights(s - PERM0)
+            if s >= PERM0 and (s - PERM0) % 4 == 0 and (s - PERM0) // 4 < 8:
+                permute_value_weights((s - PERM0) // 4)
             if 0 <= x < 80:
                 rotate(x // 4, x % 4, 0)
             if 0 <= i < LASTG:
@@ -320,13 +359,11 @@ def tile_gpt_pa_kernel(
             if 0 <= x < 80:
                 rotate(x // 4, x % 4, 1)
             if s in v_step:
-                turn_value(v_step[s], 0)
+                turn_value(v_step[s][0], v_step[s][1])
             if 0 <= i < LASTG - 1:
                 tap(i, 2)
                 if not pool_tap(i):
                     tap(i, 3)
-            if s in v_step:
-                turn_value(v_step[s], 1)
 
         for s in range(NG):
             y = s - SLAG
@@ -341,12 +378,18 @@ def tile_gpt_pa_kernel(
                 conv_weights()
             if s == 7:
                 rope_tables()
+            if s == 95:
+                empty_value(2, 2)
+                empty_value(2, 3)
+                store_rows(2, 0)
+                store_rows(2, 1)
             if s >= 1:
                 taps(s - 1)
-            if SINGLE0 <= s - 3 and pool_tap(s - 3):
-                silu_value(s - 3)
-            if SINGLE0 <= s - 2 and not pool_tap(s - 2):
-                silu_value(s - 2)
+            if SINGLE0 <= s - VLAG < 88:
+                silu_value(s - VLAG)
+            if s == 94:
+                empty_value(2, 0)
+                empty_value(2, 1)
             vector_step(s)
             if s in t_step:
                 for hh in range(4):
@@ -365,15 +408,20 @@ def tile_gpt_pa_kernel(
         tap(LASTG - 1, 2)
         tap(LASTG, 1, 0, 256)
         tap(LASTG - 1, 3)
-        silu_value(93)
         taps(LASTG, 256, 256)
-        silu_value(94)
         tap(LASTG, 2, 0, 256)
         tap(LASTG, 1, 256, 256)
         tap(LASTG, 3, 0, 256)
         tap(LASTG, 2, 256, 256)
-        silu_value(LASTG, (0,))
         tap(LASTG, 3, 256, 256)
-        turn_value(3, 0)
-        silu_value(LASTG, (1,))
-        turn_value(3, 1)
+        for m in range(3):
+            transposes(23, m, "tb")
+            empty_last(m)
+        transposes(23, 3, "tb", 0, 2)
+        empty_last(3, (0,))
+        store_rows(3, 0)
+        transposes(23, 3, "u", 2, 4)
+        empty_tile(1, 0)
+        store_rows(3, 1, 0, 1)
+        empty_tile(1, 1)
+        store_rows(3, 1, 1, 2)

@@ -57,7 +57,8 @@ def tile_gpt_pa_kernel(
             wck.append(t_wck)
             wpk.append(t_wpk)
         wch0 = keep.tile([P, PASSES, 256], U8, name="wch0", align_bytes=64)
-        wcr0 = keep.tile([P, PASSES, 768], U8, name="wcr0", align_bytes=64)
+        wch1 = keep.tile([P, PASSES, 256], U8, name="wch1", align_bytes=64)
+        wcr0 = keep.tile([P, PASSES, 512], U8, name="wcr0", align_bytes=64)
         wcv = keep.tile([P, PASSES, 1024], U8, name="wcv", align_bytes=64)
         wpv = keep.tile([P, PASSES, 512], U8, name="wpv", align_bytes=64)
         zb = keep.tile([P, 512], BF16, name="zb")
@@ -90,12 +91,6 @@ def tile_gpt_pa_kernel(
         nc.vector.memset(zb[:], 0.0)
         nc.vector.memset(wl[:], 0.0)
         nc.gpsimd.memset(zeros[:], 0.0)
-        nc.gpsimd.dma_start(out=wl[0:16, :], in_=q_conv_w.rearrange("(h p) j -> h (p j)", p=P))
-        nc.gpsimd.dma_start(out=wl[16:20, :], in_=k_conv_w.rearrange("(h p) j -> h (p j)", p=P))
-        nc.gpsimd.dma_start(
-            out=wl[20:24, :].rearrange("m (a x) -> m a x", a=4),
-            in_=v_conv_w.rearrange("(a m r) j -> m a (r j)", a=4, m=4),
-        )
         make_identity(nc, ident[:])
         nc.scalar.activation(out=scr[:, 0:1], in_=zeros[:, 0:1], func=AF.Silu)
 
@@ -103,8 +98,15 @@ def tile_gpt_pa_kernel(
         load_codes(xc[0], x_words, 0, 4, 0, 512)
         load_scales(xp[0], x_scales, 0, 512)
         load_scales(wpq[0], Wqkv_scales, 0, 512)
+        nc.sync.dma_start(out=wl[0:16, :], in_=q_conv_w.rearrange("(h p) j -> h (p j)", p=P))
+        nc.sync.dma_start(out=wl[16:20, :], in_=k_conv_w.rearrange("(h p) j -> h (p j)", p=P))
+        nc.sync.dma_start(
+            out=wl[20:24, :].rearrange("m (a x) -> m a x", a=4),
+            in_=v_conv_w.rearrange("(a m r) j -> m a (r j)", a=4, m=4),
+        )
         load_codes(xc[0], x_words, 4, 8, 0, 512)
-        load_codes(wcr0, Wqkv_words, 0, 8, 128, 512)
+        load_codes(wch1, Wqkv_words, 0, 8, 128, 256)
+        load_codes(wcr0, Wqkv_words, 0, 8, 256, 512)
 
         warm = psum.tile([P, NTOK], F32, name="tb", tag="tb", bufs=5)
         for w in range(NWARM):
@@ -166,8 +168,10 @@ def tile_gpt_pa_kernel(
             b, hh = divmod(r, 4)
             if st == 0 and hh == 0:
                 return b, wch0, 0, wpq[0], 0, 0
+            if st == 0 and hh == 1:
+                return b, wch1, 0, wpq[0], 128, 1
             if st == 0:
-                return b, wcr0, 128 * (hh - 1), wpq[0], 128 * hh, hh
+                return b, wcr0, 128 * (hh - 2), wpq[0], 128 * hh, hh
             if st < 4:
                 return b, wcq[st], 128 * hh, wpq[st], 128 * hh, 4 * st + hh
             if st == 4:

@@ -23,12 +23,12 @@ SINGLE0 = 80
 LASTG = 95
 NWARM = 14
 
-SLAG = 6
-TLAG = 9
-RLAG = 10
+SLAG = 5
+TLAG = 8
+RLAG = 9
 PLAG = 3
-ALAG = 12
-PERM0 = 22
+ALAG = 11
+PERM0 = 18
 VLAG = 5
 
 
@@ -349,13 +349,13 @@ def tile_gpt_pa_kernel(
         t_step = {93: 22}
         for un in range(20):
             t_step[4 * un + TLAG] = un
-        v_step = {90: (0, 0), 91: (0, 1), 93: (1, 0), 94: (1, 1)}
+        v_step = {89: (0, 0), 90: (0, 1), 93: (1, 0), 94: (1, 1)}
 
         def vector_step(s):
             i = s - 1
             x = s - RLAG
-            if s >= PERM0 and (s - PERM0) % 4 == 0 and (s - PERM0) // 4 < 8:
-                permute_value_weights((s - PERM0) // 4)
+            if s >= PERM0 and (s - PERM0) % 8 == 0 and (s - PERM0) // 8 < 8:
+                permute_value_weights((s - PERM0) // 8)
             if 0 <= x < 80:
                 rotate(x // 4, x % 4, 0)
             if 0 <= i < LASTG:

from contextlib import ExitStack

import concourse.mybir as mybir
from concourse.masks import make_identity

F32 = mybir.dt.float32
BF16 = mybir.dt.bfloat16
U8 = mybir.dt.uint8
I32 = mybir.dt.int32
FP4X4 = mybir.dt.float4_e2m1fn_x4
AF = mybir.ActivationFunctionType
ALU = mybir.AluOpType

FLOPS = 2 * 2048 * 4096 * 3072

P = 128
PASSES = 8
NTOK = 512
NG = 96
ACCW = 520
DIRECT0 = 94
SINGLE0 = 80
LASTG = 95
NWARM = 14

SLAG = 5
TLAG = 8
RLAG = 9
PLAG = 3
ALAG = 11
PERM0 = 18
VLAG = 5


def tile_gpt_pa_kernel(
    tc, x_words, x_scales, Wqkv_words, Wqkv_scales, q_conv_w, k_conv_w, v_conv_w, cos, sin, out_0, out_1, out_2
):
    nc = tc.nc
    with ExitStack() as ctx:
        keep = ctx.enter_context(tc.tile_pool(name="keep", bufs=1))
        work = ctx.enter_context(tc.tile_pool(name="work", bufs=2))
        psum = ctx.enter_context(tc.psum_pool(name="psum", bufs=4))
        ctx.enter_context(tc.manual_schedule())

        xc, xp, wcq, wpq, wck, wpk = [], [], [], [], [], []
        for b in range(4):
            t_xc = keep.tile([P, PASSES, 1024], U8, name="xc%d" % b, align_bytes=64)
            t_xp = keep.tile([P, PASSES, 512], U8, name="xp%d" % b, align_bytes=64)
            t_wcq = keep.tile([P, PASSES, 1024], U8, name="wcq%d" % b, align_bytes=64) if b > 0 else None
            t_wpq = keep.tile([P, PASSES, 512], U8, name="wpq%d" % b, align_bytes=64)
            t_wck = keep.tile([P, PASSES, 512], U8, name="wck%d" % b, align_bytes=64)
            t_wpk = keep.tile([P, PASSES, 256], U8, name="wpk%d" % b, align_bytes=64)
            xc.append(t_xc)
            xp.append(t_xp)
            wcq.append(t_wcq)
            wpq.append(t_wpq)
            wck.append(t_wck)
            wpk.append(t_wpk)
        wch0 = keep.tile([P, PASSES, 256], U8, name="wch0", align_bytes=64)
        wch1 = keep.tile([P, PASSES, 256], U8, name="wch1", align_bytes=64)
        wcr0 = keep.tile([P, PASSES, 512], U8, name="wcr0", align_bytes=64)
        wcv = keep.tile([P, PASSES, 1024], U8, name="wcv", align_bytes=64)
        wpv = keep.tile([P, PASSES, 512], U8, name="wpv", align_bytes=64)
        zb = keep.tile([P, 512], BF16, name="zb")
        wl = keep.tile([P, 512], BF16, name="wl")
        wd = keep.tile([P, 4, P], F32, name="wd")
        wf = keep.tile([P, 4, 24], F32, name="wf")
        craw = keep.tile([P, 16, 64], BF16, name="craw")
        sraw = keep.tile([P, 16, 64], BF16, name="sraw")
        cs1 = keep.tile([P, 16, 128], F32, name="cs1")
        cs2 = keep.tile([P, 16, 128], F32, name="cs2")
        ident = keep.tile([P, P], F32, name="ident")
        zeros = keep.tile([P, 8], F32, name="zeros")
        scr = keep.tile([P, 8], F32, name="scr")

        def load_codes(dst, src, g0, g1, n0, n1):
            nc.sync.dma_start(
                out=dst[:, g0:g1, :].bitcast(I32),
                in_=src[g0:g1, :, 2 * n0 : 2 * n1].rearrange("g p n -> p g n").bitcast(I32),
            )

        def load_scales(dst, src, n0, n1):
            for q in range(4):
                nc.sync.dma_start(
                    out=dst[32 * q : 32 * q + 4, :, :].bitcast(I32),
                    in_=src[:, 4 * q : 4 * q + 4, n0:n1].rearrange("g r n -> r g n").bitcast(I32),
                )

        nc.vector.memset(xp[0][:].bitcast(I32), 0)
        nc.gpsimd.memset(wpq[0][:].bitcast(F32), 0.0)
        nc.vector.memset(zb[:], 0.0)
        nc.vector.memset(wl[:], 0.0)
        nc.gpsimd.memset(zeros[:], 0.0)
        make_identity(nc, ident[:])
        nc.scalar.activation(out=scr[:, 0:1], in_=zeros[:, 0:1], func=AF.Silu)

        load_codes(wch0, Wqkv_words, 0, 8, 0, 128)
        load_codes(xc[0], x_words, 0, 4, 0, 512)
        load_scales(xp[0], x_scales, 0, 512)
        load_scales(wpq[0], Wqkv_scales, 0, 512)
        nc.sync.dma_start(out=wl[0:16, :], in_=q_conv_w.rearrange("(h p) j -> h (p j)", p=P))
        nc.sync.dma_start(out=wl[16:20, :], in_=k_conv_w.rearrange("(h p) j -> h (p j)", p=P))
        nc.sync.dma_start(
            out=wl[20:24, :].rearrange("m (a x) -> m a x", a=4),
            in_=v_conv_w.rearrange("(a m r) j -> m a (r j)", a=4, m=4),
        )
        load_codes(xc[0], x_words, 4, 8, 0, 512)
        load_codes(wch1, Wqkv_words, 0, 8, 128, 256)
        load_codes(wcr0, Wqkv_words, 0, 8, 256, 512)

        warm = psum.tile([P, NTOK], F32, name="tb", tag="tb", bufs=5)
        for w in range(NWARM):
            nc.tensor.matmul(out=warm[:], lhsT=zb[:, 0:P], rhs=zb[:], start=True, stop=True)

        for b in range(1, 4):
            nc.vector.memset(xp[b][:].bitcast(I32), 0)
            nc.gpsimd.memset(wpq[b][:].bitcast(F32), 0.0)
        for c in range(4):
            nc.gpsimd.memset(wpk[c][:].bitcast(F32), 0.0)
        load_scales(xp[1], x_scales, 512, 1024)
        load_codes(xc[1], x_words, 0, 8, 512, 1024)
        load_scales(xp[2], x_scales, 1024, 1536)
        load_scales(xp[3], x_scales, 1536, 2048)
        nc.sync.dma_start(out=craw[:], in_=cos.rearrange("(t p) i -> p t i", p=P))
        nc.sync.dma_start(out=sraw[:], in_=sin.rearrange("(t p) i -> p t i", p=P))
        load_codes(xc[2], x_words, 0, 8, 1024, 1536)
        load_codes(xc[3], x_words, 0, 8, 1536, 2048)
        for c in range(1, 4):
            load_scales(wpq[c], Wqkv_scales, 768 * c, 768 * c + 512)
        for c in range(4):
            load_scales(wpk[c], Wqkv_scales, 768 * c + 512, 768 * c + 768)
        for c in range(1, 4):
            load_codes(wcq[c], Wqkv_words, 0, 8, 768 * c, 768 * c + 512)
        for c in range(4):
            load_codes(wck[c], Wqkv_words, 0, 8, 768 * c + 512, 768 * c + 768)

        nc.vector.tensor_copy(out=wd[:], in_=wl[:].rearrange("h (p j) -> h j p", j=4))

        def conv_weights():
            wt = psum.tile([P, 4, P], F32, name="tb", tag="tb", bufs=5)
            for j in range(4):
                nc.tensor.transpose(out=wt[:, j, :], in_=wd[:, j, :], identity=ident[:])
            nc.vector.tensor_copy(out=wf[:], in_=wt[:, :, 0:24])

        def permute_value_weights(k):
            a = k % 4
            if k < 4:
                nc.vector.tensor_copy(
                    out=wcv[:].bitcast(I32).rearrange("p g (m a w) -> p g m a w", m=4, a=4)[:, :, :, a, :],
                    in_=wck[a][:, :, 256:512].bitcast(I32).rearrange("p g (m w) -> p g m w", m=4),
                )
            else:
                nc.vector.tensor_copy(
                    out=wpv[:].bitcast(I32).rearrange("p g (m a w) -> p g m a w", m=4, a=4)[:, :, :, a, :],
                    in_=wpk[a][:, :, 128:256].bitcast(I32).rearrange("p g (m w) -> p g m w", m=4),
                )

        def rope_tables():
            nc.scalar.copy(out=cs1[:, :, 0:64], in_=craw[:])
            nc.scalar.copy(out=cs1[:, :, 64:128], in_=sraw[:])
            nc.vector.tensor_scalar_mul(out=cs2[:, :, 0:64], in0=sraw[:], scalar1=-1.0)
            nc.vector.tensor_copy(out=cs2[:, :, 64:128], in_=craw[:])

        ubank, acc, tmp, tbank, stage, bst, vin, vout, vrow = {}, {}, {}, {}, {}, {}, {}, {}, {}

        def info(i):
            st, r = divmod(i, 16)
            b, hh = divmod(r, 4)
            if st == 0 and hh == 0:
                return b, wch0, 0, wpq[0], 0, 0
            if st == 0 and hh == 1:
                return b, wch1, 0, wpq[0], 128, 1
            if st == 0:
                return b, wcr0, 128 * (hh - 2), wpq[0], 128 * hh, hh
            if st < 4:
                return b, wcq[st], 128 * hh, wpq[st], 128 * hh, 4 * st + hh
            if st == 4:
                return b, wck[hh], 0, wpk[hh], 0, 16 + hh
            return b, wcv, 128 * hh, wpv, 128 * hh, 20 + hh

        def pool_tap(i):
            return i < 90 or 92 <= i < DIRECT0

        def project(i, lo=0, n=NTOK):
            b, codes, ccol, planes, pcol, widx = info(i)
            u = psum.tile([P, n], F32, name="u", tag="u", bufs=3)
            ubank[(i, lo)] = u
            for g in range(PASSES):
                nc.tensor.matmul_mx(
                    out=u[:],
                    lhsT=codes[:, g, 2 * ccol : 2 * ccol + 256].bitcast(FP4X4),
                    lhsT_scale=planes[:, g, pcol : pcol + 128],
                    rhs=xc[b][:, g, 2 * lo : 2 * (lo + n)].bitcast(FP4X4),
                    rhs_scale=xp[b][:, g, lo : lo + n],
                    start=(g == 0),
                    stop=(g == PASSES - 1),
                )

        def taps(i, lo=0, n=NTOK):
            b, codes, ccol, planes, pcol, widx = info(i)
            pr, e = divmod(i, 2)
            if e == 0 and lo == 0:
                a_new = work.tile([P, 2, ACCW], F32, name="acc", tag="acc", bufs=6)
                acc[pr] = a_new
                if pool_tap(i):
                    t_new = work.tile([P, 2, NTOK], F32, name="tmp", tag="tmp", bufs=3)
                    tmp[pr] = t_new
            a = acc[pr]
            u = ubank[(i, lo)]
            if lo == 0 and b == 0:
                nc.scalar.copy(out=a[:, e, 0:3], in_=zeros[:, 0:3])
            elif lo == 0:
                nc.scalar.copy(out=a[:, e, 0:3], in_=acc[pr - 2][:, e, NTOK : NTOK + 3])
            nc.scalar.activation(
                out=a[:, e, lo + 3 : lo + n + 3], in_=u[:], func=AF.Copy, scale=wf[:, 0, widx : widx + 1]
            )
            if pool_tap(i):
                nc.scalar.activation(out=tmp[pr][:, e, :], in_=u[:], func=AF.Copy, scale=wf[:, 3, widx : widx + 1])

        def tap(i, j, lo=0, n=NTOK):
            b, codes, ccol, planes, pcol, widx = info(i)
            pr, e = divmod(i, 2)
            a = acc[pr]
            sh = lo + 3 - j
            nc.vector.scalar_tensor_tensor(
                out=a[:, e, sh : sh + n],
                in0=ubank[(i, lo)][:],
                scalar=wf[:, j, widx : widx + 1],
                in1=a[:, e, sh : sh + n],
                op0=ALU.mult,
                op1=ALU.add,
            )

        def pool_add(pr):
            nc.gpsimd.tensor_tensor(out=acc[pr][:, :, 0:NTOK], in0=acc[pr][:, :, 0:NTOK], in1=tmp[pr][:], op=ALU.add)

        def pool_add_one(i):
            pr, e = divmod(i, 2)
            nc.gpsimd.tensor_tensor(out=acc[pr][:, e, 0:NTOK], in0=acc[pr][:, e, 0:NTOK], in1=tmp[pr][:, e, :], op=ALU.add)

        def silu_pair(pr):
            nc.scalar.activation(out=acc[pr][:, :, 0:NTOK], in_=acc[pr][:, :, 0:NTOK], func=AF.Silu)

        def silu_value(i, halves=(0, 1)):
            pr, e = divmod(i, 2)
            b, m = divmod(i - SINGLE0, 4)
            for hf in halves:
                if (b, hf) not in vin:
                    v_new = work.tile([P, 8, 4, 32], F32, name="stage", tag="stage", bufs=6, align_bytes=64)
                    vin[(b, hf)] = v_new
                nc.scalar.activation(
                    out=vin[(b, hf)][:, :, m, :],
                    in_=acc[pr][:, e, 256 * hf : 256 * hf + 256].rearrange("p (k c) -> p k c", c=32),
                    func=AF.Silu,
                )

        def turn_value(b, hf):
            o_new = work.tile([P, 8, 4, 32], F32, name="bst", tag="bst", bufs=4, align_bytes=64)
            vout[(b, hf)] = o_new
            nc.vector.transpose(
                out=o_new[:].rearrange("p k m r -> p (k m r)"), in_=vin[(b, hf)][:].rearrange("p k m c -> p (k m c)")
            )
            r0 = NTOK * b + 256 * hf
            for a in range(4):
                nc.sync.dma_start(
                    out=out_2[0, r0 : r0 + 256, a, :].rearrange("(k c) d -> c k d", c=32),
                    in_=o_new[32 * a : 32 * a + 32, :, :, :].rearrange("c k m r -> c k (m r)"),
                )

        def empty_value(b, m):
            for half in (0, 1):
                if (b, half) not in vrow:
                    r_new = work.tile([P, 2, 4, 4, 32], F32, name="stage", tag="stage", bufs=6, align_bytes=64)
                    vrow[(b, half)] = r_new
                nc.scalar.activation(
                    out=vrow[(b, half)][:, :, :, m, :],
                    in_=tbank[(20 + b, m, 0)][:, 2 * half : 2 * half + 2, :].rearrange("p t (a r) -> p t a r", a=4),
                    func=AF.Silu,
                )

        def empty_last(m, halves=(0, 1)):
            for half in halves:
                if (3, half) not in vrow:
                    r_new = work.tile([P, 2, 4, 4, 32], F32, name="stage", tag="stage", bufs=6, align_bytes=64)
                    vrow[(3, half)] = r_new
                if m < 3:
                    src = tbank[(23, m, 0)][:, 2 * half : 2 * half + 2, :]
                else:
                    src = tbank[(23, m, 2 * half)][:]
                nc.scalar.activation(
                    out=vrow[(3, half)][:, :, :, m, :], in_=src.rearrange("p t (a r) -> p t a r", a=4), func=AF.Silu
                )

        def store_rows(b, half, t0=0, t1=2):
            r0 = NTOK * b + 256 * half
            nc.sync.dma_start(
                out=out_2[0, r0 + P * t0 : r0 + P * t1, :, :].rearrange("(t p) a d -> p t (a d)", p=P),
                in_=vrow[(b, half)][:, t0:t1, :, :, :].rearrange("p t a m r -> p t (a m r)"),
            )

        def empty_tile(half, tt):
            nc.scalar.activation(
                out=vrow[(3, half)][:, tt : tt + 1, :, 3, :],
                in_=tbank[(23, 3, 2 * half)][:, tt : tt + 1, :].rearrange("p t (a r) -> p t a r", a=4),
                func=AF.Silu,
            )

        def transposes(un, hh, tag, t0=0, t1=4):
            tb = psum.tile([P, t1 - t0, P], F32, name=tag, tag=tag, bufs=(3 if tag == "u" else 5))
            tbank[(un, hh, t0)] = tb
            a = acc[2 * un + hh // 2]
            for tt in range(t0, t1):
                nc.tensor.transpose(out=tb[:, tt - t0, :], in_=a[:, hh % 2, P * tt : P * (tt + 1)], identity=ident[:])

        def rotate(un, hh, half):
            key, e = (un, hh // 2), hh % 2
            if key not in stage:
                s_new = work.tile([P, 4, 2, P], F32, name="stage", tag="stage", bufs=6, align_bytes=64)
                stage[key] = s_new
                b_new = work.tile([P, 4, 2, P], F32, name="bst", tag="bst", bufs=4, align_bytes=64)
                bst[key] = b_new
            tts = slice(4 * (un % 4), 4 * (un % 4) + 4)
            nc.vector.tensor_tensor(
                out=(bst if half else stage)[key][:, :, e, :].rearrange("p t (r i) -> p t r i", r=2),
                in0=tbank[(un, hh, 0)][:, :, 64 * half : 64 * half + 64].unsqueeze(2).to_broadcast([P, 4, 2, 64]),
                in1=(cs2 if half else cs1)[:, tts, :].rearrange("p t (r i) -> p t r i", r=2),
                op=ALU.mult,
            )

        def rope_add(un, half):
            nc.gpsimd.tensor_tensor(out=stage[(un, half)][:], in0=stage[(un, half)][:], in1=bst[(un, half)][:], op=ALU.add)

        def store(un, part, t0=0, t1=4):
            st, b = divmod(un, 4)
            width = 1 if un >= 20 else 2
            rows = slice(NTOK * b + P * t0, NTOK * b + P * t1)
            h0 = width * part
            if st < 4:
                dst = out_0[0, rows, 4 * st + h0 : 4 * st + h0 + width, :]
            elif st == 4:
                dst = out_1[0, rows, h0 : h0 + width, :]
            else:
                dst = out_2[0, rows, h0 : h0 + width, :]
            nc.sync.dma_start(
                out=dst.rearrange("(tt p) h d -> p tt (h d)", p=P),
                in_=stage[(un, part)][:, t0:t1, :, :].rearrange("p tt h d -> p tt (h d)"),
            )

        t_step = {93: 22}
        for un in range(20):
            t_step[4 * un + TLAG] = un
        v_step = {89: (0, 0), 90: (0, 1), 93: (1, 0), 94: (1, 1)}

        def vector_step(s):
            i = s - 1
            x = s - RLAG
            if s >= PERM0 and (s - PERM0) % 8 == 0 and (s - PERM0) // 8 < 8:
                permute_value_weights((s - PERM0) // 8)
            if 0 <= x < 80:
                rotate(x // 4, x % 4, 0)
            if 0 <= i < LASTG:
                tap(i, 1)
            if 0 <= x < 80:
                rotate(x // 4, x % 4, 1)
            if s in v_step:
                turn_value(v_step[s][0], v_step[s][1])
            if 0 <= i < LASTG - 1:
                tap(i, 2)
                if not pool_tap(i):
                    tap(i, 3)

        for s in range(NG):
            y = s - SLAG
            if y >= 0 and y % 2 == 0 and y < SINGLE0:
                silu_pair(y // 2)
            if s < LASTG:
                project(s)
            else:
                project(s, 0, 256)
                project(s, 256, 256)
            if s == 0:
                conv_weights()
            if s == 7:
                rope_tables()
            if s == 95:
                empty_value(2, 2)
                empty_value(2, 3)
                store_rows(2, 0)
                store_rows(2, 1)
            if s >= 1:
                taps(s - 1)
            if SINGLE0 <= s - VLAG < 88:
                silu_value(s - VLAG)
            if s == 94:
                empty_value(2, 0)
                empty_value(2, 1)
            vector_step(s)
            if s in t_step:
                for hh in range(4):
                    transposes(t_step[s], hh, "tb")
            y = s - PLAG
            if y >= 0 and y % 2 == 0 and y < SINGLE0:
                pool_add(y // 2)
            if SINGLE0 <= s - 2 and pool_tap(s - 2):
                pool_add_one(s - 2)
            y = s - ALAG
            if y >= 0 and y % 2 == 0 and y // 4 < 20:
                rope_add(y // 4, (y % 4) // 2)
                store(y // 4, (y % 4) // 2)

        taps(LASTG, 0, 256)
        tap(LASTG - 1, 2)
        tap(LASTG, 1, 0, 256)
        tap(LASTG - 1, 3)
        taps(LASTG, 256, 256)
        tap(LASTG, 2, 0, 256)
        tap(LASTG, 1, 256, 256)
        tap(LASTG, 3, 0, 256)
        tap(LASTG, 2, 256, 256)
        tap(LASTG, 3, 256, 256)
        for m in range(3):
            transposes(23, m, "tb")
            empty_last(m)
        transposes(23, 3, "tb", 0, 2)
        empty_last(3, (0,))
        store_rows(3, 0)
        transposes(23, 3, "u", 2, 4)
        empty_tile(1, 0)
        store_rows(3, 1, 0, 1)
        empty_tile(1, 1)
        store_rows(3, 1, 1, 2)
